import numpy as np
import ml_dtypes

BF16 = ml_dtypes.bfloat16


def bf(x):
    return np.asarray(x, np.float32).astype(BF16)


def f32(x):
    return np.asarray(x, np.float32)


def f64(x):
    return np.asarray(x).astype(np.float64)


def striped(idx):
    return np.tile(idx.reshape(-1, 16).T, (8, 1))


C, H, S, N = 512, 2, 2048, 1024
EPS, NEG_SLOPE, A_W, A_B, XS = 1e-5, 0.01, 0.25, 0.15, 0.14


def setup_inputs():
    return {"base": f32(np.random.standard_normal((C, S))), "x": bf(XS * np.random.standard_normal((C, N))), "w": bf(np.random.standard_normal((C, H * C)) / np.sqrt(C)), "offs": striped(np.random.permutation(S)[:N])}


def reference(base, x, w, offs):
    idx = offs[:16].T.reshape(-1)
    xf = f64(x)
    p = f64(w).T @ xf
    wh, ws = p[:C], p[C:]
    t = np.tanh(wh + ws + (A_W + A_B))
    sc = t.T @ wh
    e = np.exp(sc - sc.max(axis=1, keepdims=True))
    attn = e / e.sum(axis=1, keepdims=True)
    o = wh @ attn.T + xf
    d = o - o.mean(axis=1, keepdims=True)
    z = d / np.sqrt((d * d).mean(axis=1, keepdims=True) + EPS)
    slope = np.where(z >= 0, 1.0, NEG_SLOPE)
    out = f64(base).copy()
    out[:, idx] = z * slope
    return out

@@ -1,0 +1,189 @@
+import concourse.mybir as mybir
+from concourse.masks import make_identity
+
+BF16, F32, U16 = mybir.dt.bfloat16, mybir.dt.float32, mybir.dt.uint16
+ALU = mybir.AluOpType
+ACT = mybir.ActivationFunctionType
+
+P = 128
+C = 512
+N = 1024
+S = 2048
+CB = C // P
+NB = N // P
+HALF = 512
+QB = HALF // P
+BIAS = 0.25 + 0.15
+EPS = 1e-5
+NEG_SLOPE = 0.01
+AHEAD = 2
+
+FLOPS = 3 * 2 * C * N * N
+
+
+def tile_gatconv_b_kernel(tc, base, x, w, offs, out):
+    nc = tc.nc
+    base_rows = base.rearrange("(cb p) s -> cb p s", p=P)
+    out_rows = out.rearrange("(cb p) s -> cb p s", p=P)
+    x_rows = x.rearrange("(kb p) j -> kb p j", p=P)
+    w_rows = w.rearrange("(kb p) m -> kb p m", p=P)
+
+    with (
+        tc.tile_pool(name="held", bufs=1) as held,
+        tc.tile_pool(name="work", bufs=2) as work,
+        tc.tile_pool(name="soft", bufs=AHEAD + 1) as soft,
+        tc.tile_pool(name="stat", bufs=4) as stat,
+        tc.psum_pool(name="acc", bufs=3) as acc,
+        tc.psum_pool(name="flip", bufs=2) as flip,
+    ):
+        offsets = held.tile([P, N // 16], U16, name="offsets")
+        nc.sync.dma_start(offsets[:], offs)
+        x_bf = [held.tile([P, N], BF16, name=f"x_bf{kb}") for kb in range(CB)]
+        w_bf = [held.tile([P, 2 * C], BF16, name=f"w_bf{kb}") for kb in range(CB)]
+        for kb in range(CB):
+            nc.sync.dma_start(x_bf[kb][:], x_rows[kb])
+            nc.scalar.dma_start(w_bf[kb][:], w_rows[kb])
+        window = [held.tile([P, S], F32, name=f"window{cb}") for cb in range(CB)]
+        for cb in range(CB):
+            queue = nc.sync if cb % 2 == 0 else nc.scalar
+            queue.dma_start(window[cb][:], base_rows[cb])
+
+        ident = held.tile([P, P], BF16, name="ident")
+        make_identity(nc, ident[:])
+        tanh_bias = held.tile([P, 1], F32, name="tanh_bias")
+        nc.vector.memset(tanh_bias[:], BIAS)
+        neg_half = held.tile([P, 1], F32, name="neg_half")
+        nc.vector.memset(neg_half[:], -0.5)
+
+        wh_bf = [held.tile([P, N], BF16, name=f"wh_bf{cb}") for cb in range(CB)]
+        t_bf = [held.tile([P, N], BF16, name=f"t_bf{cb}") for cb in range(CB)]
+        whT = held.tile([P, NB, C], BF16, name="whT")
+        attnT = [held.tile([P, NB, HALF], BF16, name=f"attnT{jh}") for jh in range(2)]
+
+        def project(jh, cb):
+            cols = slice(jh * HALF, (jh + 1) * HALF)
+            p_ps = acc.tile([P, 2 * HALF], F32, name="p_ps", tag="acc")
+            for part in range(2):
+                for kb in range(CB):
+                    nc.tensor.matmul(
+                        p_ps[:, part * HALF : (part + 1) * HALF],
+                        lhsT=w_bf[kb][:, part * C + cb * P : part * C + (cb + 1) * P],
+                        rhs=x_bf[kb][:, cols],
+                        start=(kb == 0),
+                        stop=(kb == CB - 1),
+                    )
+            wh_f = work.tile([P, HALF], F32, name="wh_f")
+            nc.scalar.copy(wh_f[:], p_ps[:, 0:HALF])
+            arg = work.tile([P, HALF], F32, name="arg")
+            nc.vector.tensor_tensor(arg[:], p_ps[:, HALF : 2 * HALF], wh_f[:], ALU.add)
+            nc.vector.tensor_copy(wh_bf[cb][:, cols], wh_f[:])
+            nc.scalar.activation(t_bf[cb][:, cols], arg[:], ACT.Tanh, bias=tanh_bias[:])
+
+        def flip_wh(jh, cb):
+            whT_ps = flip.tile([P, NB, P], BF16, name="whT_ps", tag="flip")
+            for q in range(QB):
+                nb = jh * QB + q
+                nc.tensor.transpose(whT_ps[:, q, :], wh_bf[cb][:, nb * P : (nb + 1) * P], ident[:])
+            nc.vector.tensor_copy(whT[:, jh * QB : (jh + 1) * QB, cb * P : (cb + 1) * P], whT_ps[:, 0:QB, :])
+
+        units = [(jh, cb) for jh in range(2) for cb in range(CB)]
+        for u, unit in enumerate(units):
+            project(*unit)
+            if u >= 1:
+                flip_wh(*units[u - 1])
+        flip_wh(*units[-1])
+
+        def scores(jb):
+            sc_ps = acc.tile([P, N], F32, name="sc_ps", tag="acc")
+            for nh in range(2):
+                for cb in range(CB):
+                    nc.tensor.matmul(
+                        sc_ps[:, nh * HALF : (nh + 1) * HALF],
+                        lhsT=t_bf[cb][:, jb * P : (jb + 1) * P],
+                        rhs=wh_bf[cb][:, nh * HALF : (nh + 1) * HALF],
+                        start=(cb == 0),
+                        stop=(cb == CB - 1),
+                    )
+            top2 = stat.tile([P, 2], F32, name="top2")
+            for nh in range(2):
+                nc.vector.reduce_max(top2[:, nh : nh + 1], sc_ps[:, nh * HALF : (nh + 1) * HALF], axis=mybir.AxisListType.X)
+            neg_top = stat.tile([P, 1], F32, name="neg_top")
+            nc.vector.tensor_scalar(neg_top[:], top2[:, 0:1], top2[:, 1:2], -1.0, op0=ALU.max, op1=ALU.mult)
+            e_f = soft.tile([P, N], F32, name="e_f")
+            sum2 = stat.tile([P, 2], F32, name="sum2")
+            for nh in range(2):
+                nc.scalar.activation(
+                    e_f[:, nh * HALF : (nh + 1) * HALF],
+                    sc_ps[:, nh * HALF : (nh + 1) * HALF],
+                    ACT.Exp,
+                    bias=neg_top[:],
+                    accum_out=sum2[:, nh : nh + 1],
+                )
+            total = stat.tile([P, 1], F32, name="total")
+            nc.vector.tensor_tensor(total[:], sum2[:, 0:1], sum2[:, 1:2], ALU.add)
+            rinv = stat.tile([P, 1], F32, name="rinv")
+            nc.vector.reciprocal(rinv[:], total[:])
+            attn_bf = soft.tile([P, N], BF16, name="attn_bf")
+            nc.gpsimd.tensor_scalar(attn_bf[:], e_f[:], rinv[:], 1.0, op0=ALU.mult, op1=ALU.mult)
+            return attn_bf
+
+        def flip_attn(jb, attn_bf):
+            aT_ps = flip.tile([P, NB, P], BF16, name="aT_ps", tag="flip")
+            for nb in range(NB):
+                nc.tensor.transpose(aT_ps[:, nb, :], attn_bf[:, nb * P : (nb + 1) * P], ident[:])
+            jh, q = divmod(jb, QB)
+            nc.vector.tensor_copy(attnT[jh][:, :, q * P : (q + 1) * P], aT_ps[:])
+
+        def attend(o_ps, cb, jh):
+            cols = slice(jh * HALF, (jh + 1) * HALF)
+            for nb in range(NB):
+                nc.tensor.matmul(
+                    o_ps[:, cols],
+                    lhsT=whT[:, nb, cb * P : (cb + 1) * P],
+                    rhs=attnT[jh][:, nb, :],
+                    start=(nb == 0),
+                    stop=False,
+                )
+            nc.tensor.matmul(o_ps[:, cols], lhsT=ident[:], rhs=x_bf[cb][:, cols], start=False, stop=True)
+
+        def place(o_ps, cb):
+            o_sb = work.tile([P, N], F32, name="o_sb")
+            osum2 = stat.tile([P, 2], F32, name="osum2")
+            for jh in range(2):
+                cols = slice(jh * HALF, (jh + 1) * HALF)
+                nc.scalar.activation(o_sb[:, cols], o_ps[:, cols], ACT.Identity, accum_out=osum2[:, jh : jh + 1])
+            scaled2 = stat.tile([P, 2], F32, name="scaled2")
+            mean = stat.tile([P, 1], F32, name="mean")
+            nc.scalar.activation(scaled2[:], osum2[:], ACT.Identity, scale=1.0 / N, accum_out=mean[:])
+            slope = work.tile([P, N], F32, name="slope")
+            nc.gpsimd.tensor_scalar(slope[:], o_sb[:], mean[:], NEG_SLOPE, op0=ALU.is_ge, op1=ALU.max)
+            squares = work.tile([P, N], F32, name="squares")
+            ssq = stat.tile([P, 1], F32, name="ssq")
+            nc.scalar.activation(squares[:], o_sb[:], ACT.Square, bias=mean[:], scale=-1.0, accum_out=ssq[:])
+            var_eps = stat.tile([P, 1], F32, name="var_eps")
+            nc.gpsimd.tensor_scalar(var_eps[:], ssq[:], 1.0 / N, EPS, op0=ALU.mult, op1=ALU.add)
+            rstd = stat.tile([P, 1], F32, name="rstd")
+            nc.gpsimd.tensor_tensor(rstd[:], var_eps[:], neg_half[:], ALU.pow)
+            shift = stat.tile([P, 1], F32, name="shift")
+            nc.gpsimd.tensor_scalar(shift[:], mean[:], rstd[:], -1.0, op0=ALU.mult, op1=ALU.mult)
+            z = work.tile([P, N], F32, name="z")
+            nc.scalar.activation(z[:], o_sb[:], ACT.Identity, bias=shift[:], scale=rstd[:])
+            nc.vector.tensor_tensor(window[cb][:].indirect(offsets[:]), z[:], slope[:], ALU.mult)
+            nc.sync.dma_start(out_rows[cb], window[cb][:])
+
+        waiting = {}
+        for jb in range(NB):
+            waiting[jb] = scores(jb)
+            if jb >= AHEAD:
+                flip_attn(jb - AHEAD, waiting.pop(jb - AHEAD))
+        o_first = acc.tile([P, N], F32, name="o_first", tag="acc")
+        attend(o_first, 0, 0)
+        for jb in range(NB - AHEAD, NB):
+            flip_attn(jb, waiting.pop(jb))
+        attend(o_first, 0, 1)
+        place(o_first, 0)
+        for cb in range(1, CB):
+            o_ps = acc.tile([P, N], F32, name="o_ps", tag="acc")
+            attend(o_ps, cb, 0)
+            attend(o_ps, cb, 1)
+            place(o_ps, cb)

@@ -153,21 +153,23 @@ def tile_gatconv_b_kernel(tc, base, x, w, offs, out):
                 cols = slice(jh * HALF, (jh + 1) * HALF)
                 nc.scalar.activation(o_sb[:, cols], o_ps[:, cols], ACT.Identity, accum_out=osum2[:, jh : jh + 1])
             scaled2 = stat.tile([P, 2], F32, name="scaled2")
-            mean = stat.tile([P, 1], F32, name="mean")
-            nc.scalar.activation(scaled2[:], osum2[:], ACT.Identity, scale=1.0 / N, accum_out=mean[:])
-            slope = work.tile([P, N], F32, name="slope")
-            nc.gpsimd.tensor_scalar(slope[:], o_sb[:], mean[:], NEG_SLOPE, op0=ALU.is_ge, op1=ALU.max)
+            neg_mean = stat.tile([P, 1], F32, name="neg_mean")
+            nc.scalar.activation(scaled2[:], osum2[:], ACT.Identity, scale=-1.0 / N, accum_out=neg_mean[:])
             squares = work.tile([P, N], F32, name="squares")
             ssq = stat.tile([P, 1], F32, name="ssq")
-            nc.scalar.activation(squares[:], o_sb[:], ACT.Square, bias=mean[:], scale=-1.0, accum_out=ssq[:])
+            nc.scalar.activation(squares[:], o_sb[:], ACT.Square, bias=neg_mean[:], accum_out=ssq[:])
+            sign = work.tile([P, N], F32, name="sign")
+            nc.scalar.activation(sign[:], o_sb[:], ACT.Sign, bias=neg_mean[:])
             var_eps = stat.tile([P, 1], F32, name="var_eps")
             nc.gpsimd.tensor_scalar(var_eps[:], ssq[:], 1.0 / N, EPS, op0=ALU.mult, op1=ALU.add)
             rstd = stat.tile([P, 1], F32, name="rstd")
             nc.gpsimd.tensor_tensor(rstd[:], var_eps[:], neg_half[:], ALU.pow)
             shift = stat.tile([P, 1], F32, name="shift")
-            nc.gpsimd.tensor_scalar(shift[:], mean[:], rstd[:], -1.0, op0=ALU.mult, op1=ALU.mult)
+            nc.gpsimd.tensor_tensor(shift[:], neg_mean[:], rstd[:], ALU.mult)
             z = work.tile([P, N], F32, name="z")
             nc.scalar.activation(z[:], o_sb[:], ACT.Identity, bias=shift[:], scale=rstd[:])
+            slope = work.tile([P, N], F32, name="slope")
+            nc.gpsimd.tensor_scalar(slope[:], sign[:], 1.0, NEG_SLOPE, op0=ALU.min, op1=ALU.max)
             nc.vector.tensor_tensor(window[cb][:].indirect(offsets[:]), z[:], slope[:], ALU.mult)
             nc.sync.dma_start(out_rows[cb], window[cb][:])
 

@@ -17,6 +17,7 @@ BIAS = 0.25 + 0.15
 EPS = 1e-5
 NEG_SLOPE = 0.01
 AHEAD = 2
+PIECES = ((0, QB), (QB, QB - 1), (NB - 1, 1))
 
 FLOPS = 3 * 2 * C * N * N
 
@@ -33,80 +34,83 @@ def tile_gatconv_b_kernel(tc, base, x, w, offs, out):
         tc.tile_pool(name="work", bufs=2) as work,
         tc.tile_pool(name="soft", bufs=AHEAD + 1) as soft,
         tc.tile_pool(name="stat", bufs=4) as stat,
-        tc.psum_pool(name="acc", bufs=3) as acc,
+        tc.psum_pool(name="banks", bufs=6) as banks,
         tc.psum_pool(name="flip", bufs=2) as flip,
     ):
+        def bank(name):
+            return banks.tile([P, HALF], F32, name=name, tag="bank")
+
         offsets = held.tile([P, N // 16], U16, name="offsets")
         nc.sync.dma_start(offsets[:], offs)
-        x_bf = [held.tile([P, N], BF16, name=f"x_bf{kb}") for kb in range(CB)]
-        w_bf = [held.tile([P, 2 * C], BF16, name=f"w_bf{kb}") for kb in range(CB)]
-        for kb in range(CB):
-            nc.sync.dma_start(x_bf[kb][:], x_rows[kb])
-            nc.scalar.dma_start(w_bf[kb][:], w_rows[kb])
+        x_bf = [[held.tile([P, HALF], BF16, name=f"x_bf{jh}_{kb}") for kb in range(CB)] for jh in range(2)]
+        w_bf = [[held.tile([P, C], BF16, name=f"w_bf{part}_{kb}") for kb in range(CB)] for part in range(2)]
         window = [held.tile([P, S], F32, name=f"window{cb}") for cb in range(CB)]
-        for cb in range(CB):
-            queue = nc.sync if cb % 2 == 0 else nc.scalar
-            queue.dma_start(window[cb][:], base_rows[cb])
+        loads = []
+        for kb in range(CB):
+            loads.append((x_bf[0][kb], x_rows[kb][:, 0:HALF]))
+            loads.append((w_bf[0][kb], w_rows[kb][:, 0:C]))
+        loads += [(w_bf[1][kb], w_rows[kb][:, C : 2 * C]) for kb in range(CB)]
+        loads += [(x_bf[1][kb], x_rows[kb][:, HALF:N]) for kb in range(CB)]
+        loads += [(window[cb], base_rows[cb]) for cb in range(CB)]
+        for i, (tile, source) in enumerate(loads):
+            queue = nc.sync if i % 2 == 0 else nc.scalar
+            queue.dma_start(tile[:], source)
 
         ident = held.tile([P, P], BF16, name="ident")
         make_identity(nc, ident[:])
         tanh_bias = held.tile([P, 1], F32, name="tanh_bias")
         nc.vector.memset(tanh_bias[:], BIAS)
-        neg_half = held.tile([P, 1], F32, name="neg_half")
-        nc.vector.memset(neg_half[:], -0.5)
+        eps = held.tile([P, 1], F32, name="eps")
+        nc.vector.memset(eps[:], EPS)
 
-        wh_bf = [held.tile([P, N], BF16, name=f"wh_bf{cb}") for cb in range(CB)]
-        t_bf = [held.tile([P, N], BF16, name=f"t_bf{cb}") for cb in range(CB)]
+        wh_bf = [[held.tile([P, HALF], BF16, name=f"wh_bf{nh}_{cb}") for cb in range(CB)] for nh in range(2)]
+        t_bf = [[held.tile([P, HALF], BF16, name=f"t_bf{jh}_{cb}") for cb in range(CB)] for jh in range(2)]
         whT = held.tile([P, NB, C], BF16, name="whT")
         attnT = [held.tile([P, NB, HALF], BF16, name=f"attnT{jh}") for jh in range(2)]
 
         def project(jh, cb):
-            cols = slice(jh * HALF, (jh + 1) * HALF)
-            p_ps = acc.tile([P, 2 * HALF], F32, name="p_ps", tag="acc")
+            p_ps = [bank("wh_ps"), bank("ws_ps")]
             for part in range(2):
                 for kb in range(CB):
                     nc.tensor.matmul(
-                        p_ps[:, part * HALF : (part + 1) * HALF],
-                        lhsT=w_bf[kb][:, part * C + cb * P : part * C + (cb + 1) * P],
-                        rhs=x_bf[kb][:, cols],
+                        p_ps[part][:],
+                        lhsT=w_bf[part][kb][:, cb * P : (cb + 1) * P],
+                        rhs=x_bf[jh][kb][:],
                         start=(kb == 0),
                         stop=(kb == CB - 1),
                     )
             wh_f = work.tile([P, HALF], F32, name="wh_f")
-            nc.scalar.copy(wh_f[:], p_ps[:, 0:HALF])
+            nc.scalar.copy(wh_f[:], p_ps[0][:])
             arg = work.tile([P, HALF], F32, name="arg")
-            nc.vector.tensor_tensor(arg[:], p_ps[:, HALF : 2 * HALF], wh_f[:], ALU.add)
-            nc.vector.tensor_copy(wh_bf[cb][:, cols], wh_f[:])
-            nc.scalar.activation(t_bf[cb][:, cols], arg[:], ACT.Tanh, bias=tanh_bias[:])
+            nc.vector.tensor_tensor(arg[:], p_ps[1][:], wh_f[:], ALU.add)
+            nc.vector.tensor_copy(wh_bf[jh][cb][:], wh_f[:])
+            nc.scalar.activation(t_bf[jh][cb][:], arg[:], ACT.Tanh, bias=tanh_bias[:])
 
-        def flip_wh(jh, cb):
+        def flip_wh(cb):
             whT_ps = flip.tile([P, NB, P], BF16, name="whT_ps", tag="flip")
-            for q in range(QB):
-                nb = jh * QB + q
-                nc.tensor.transpose(whT_ps[:, q, :], wh_bf[cb][:, nb * P : (nb + 1) * P], ident[:])
-            nc.vector.tensor_copy(whT[:, jh * QB : (jh + 1) * QB, cb * P : (cb + 1) * P], whT_ps[:, 0:QB, :])
+            for nb in range(NB):
+                nh, q = divmod(nb, QB)
+                nc.tensor.transpose(whT_ps[:, nb, :], wh_bf[nh][cb][:, q * P : (q + 1) * P], ident[:])
+            nc.vector.tensor_copy(whT[:, :, cb * P : (cb + 1) * P], whT_ps[:])
 
-        units = [(jh, cb) for jh in range(2) for cb in range(CB)]
-        for u, unit in enumerate(units):
-            project(*unit)
-            if u >= 1:
-                flip_wh(*units[u - 1])
-        flip_wh(*units[-1])
+        for jh in range(2):
+            for cb in range(CB):
+                project(jh, cb)
 
         def scores(jb):
-            sc_ps = acc.tile([P, N], F32, name="sc_ps", tag="acc")
+            jh, q = divmod(jb, QB)
+            sc_ps = [bank("sc_ps0"), bank("sc_ps1")]
+            top2 = stat.tile([P, 2], F32, name="top2")
             for nh in range(2):
                 for cb in range(CB):
                     nc.tensor.matmul(
-                        sc_ps[:, nh * HALF : (nh + 1) * HALF],
-                        lhsT=t_bf[cb][:, jb * P : (jb + 1) * P],
-                        rhs=wh_bf[cb][:, nh * HALF : (nh + 1) * HALF],
+                        sc_ps[nh][:],
+                        lhsT=t_bf[jh][cb][:, q * P : (q + 1) * P],
+                        rhs=wh_bf[nh][cb][:],
                         start=(cb == 0),
                         stop=(cb == CB - 1),
                     )
-            top2 = stat.tile([P, 2], F32, name="top2")
-            for nh in range(2):
-                nc.vector.reduce_max(top2[:, nh : nh + 1], sc_ps[:, nh * HALF : (nh + 1) * HALF], axis=mybir.AxisListType.X)
+                nc.vector.reduce_max(top2[:, nh : nh + 1], sc_ps[nh][:], axis=mybir.AxisListType.X)
             neg_top = stat.tile([P, 1], F32, name="neg_top")
             nc.vector.tensor_scalar(neg_top[:], top2[:, 0:1], top2[:, 1:2], -1.0, op0=ALU.max, op1=ALU.mult)
             e_f = soft.tile([P, N], F32, name="e_f")
@@ -114,7 +118,7 @@ def tile_gatconv_b_kernel(tc, base, x, w, offs, out):
             for nh in range(2):
                 nc.scalar.activation(
                     e_f[:, nh * HALF : (nh + 1) * HALF],
-                    sc_ps[:, nh * HALF : (nh + 1) * HALF],
+                    sc_ps[nh][:],
                     ACT.Exp,
                     bias=neg_top[:],
                     accum_out=sum2[:, nh : nh + 1],
@@ -124,68 +128,76 @@ def tile_gatconv_b_kernel(tc, base, x, w, offs, out):
             rinv = stat.tile([P, 1], F32, name="rinv")
             nc.vector.reciprocal(rinv[:], total[:])
             attn_bf = soft.tile([P, N], BF16, name="attn_bf")
-            nc.gpsimd.tensor_scalar(attn_bf[:], e_f[:], rinv[:], 1.0, op0=ALU.mult, op1=ALU.mult)
-            return attn_bf
+            nc.vector.tensor_scalar(attn_bf[:], e_f[:], rinv[:], None, op0=ALU.mult)
+            return attn_bf, total
 
         def flip_attn(jb, attn_bf):
+            jh, q = divmod(jb, QB)
             aT_ps = flip.tile([P, NB, P], BF16, name="aT_ps", tag="flip")
             for nb in range(NB):
                 nc.tensor.transpose(aT_ps[:, nb, :], attn_bf[:, nb * P : (nb + 1) * P], ident[:])
-            jh, q = divmod(jb, QB)
-            nc.vector.tensor_copy(attnT[jh][:, :, q * P : (q + 1) * P], aT_ps[:])
+            if jb % 2 == 0:
+                nc.scalar.copy(attnT[jh][:, :, q * P : (q + 1) * P], aT_ps[:])
+            else:
+                nc.vector.tensor_copy(attnT[jh][:, :, q * P : (q + 1) * P], aT_ps[:])
 
-        def attend(o_ps, cb, jh):
-            cols = slice(jh * HALF, (jh + 1) * HALF)
+        def attend(cb, piece):
+            first_jb, blocks = piece
+            jh, q = divmod(first_jb, QB)
+            in_half = slice(q * P, (q + blocks) * P)
+            o_ps = bank("o_ps")
             for nb in range(NB):
                 nc.tensor.matmul(
-                    o_ps[:, cols],
+                    o_ps[:, 0 : blocks * P],
                     lhsT=whT[:, nb, cb * P : (cb + 1) * P],
-                    rhs=attnT[jh][:, nb, :],
+                    rhs=attnT[jh][:, nb, in_half],
                     start=(nb == 0),
                     stop=False,
                 )
-            nc.tensor.matmul(o_ps[:, cols], lhsT=ident[:], rhs=x_bf[cb][:, cols], start=False, stop=True)
+            nc.tensor.matmul(o_ps[:, 0 : blocks * P], lhsT=ident[:], rhs=x_bf[jh][cb][:, in_half], start=False, stop=True)
+            return o_ps
 
-        def place(o_ps, cb):
+        def place(cb, o_pieces):
             o_sb = work.tile([P, N], F32, name="o_sb")
-            osum2 = stat.tile([P, 2], F32, name="osum2")
-            for jh in range(2):
-                cols = slice(jh * HALF, (jh + 1) * HALF)
-                nc.scalar.activation(o_sb[:, cols], o_ps[:, cols], ACT.Identity, accum_out=osum2[:, jh : jh + 1])
-            scaled2 = stat.tile([P, 2], F32, name="scaled2")
+            osums = stat.tile([P, len(PIECES)], F32, name="osums")
+            for i, (first_jb, blocks) in enumerate(PIECES):
+                nc.scalar.activation(
+                    o_sb[:, first_jb * P : (first_jb + blocks) * P],
+                    o_pieces[i][:, 0 : blocks * P],
+                    ACT.Identity,
+                    accum_out=osums[:, i : i + 1],
+                )
+            scaled = stat.tile([P, len(PIECES)], F32, name="scaled")
             neg_mean = stat.tile([P, 1], F32, name="neg_mean")
-            nc.scalar.activation(scaled2[:], osum2[:], ACT.Identity, scale=-1.0 / N, accum_out=neg_mean[:])
+            nc.scalar.activation(scaled[:], osums[:], ACT.Identity, scale=-1.0 / N, accum_out=neg_mean[:])
             squares = work.tile([P, N], F32, name="squares")
             ssq = stat.tile([P, 1], F32, name="ssq")
             nc.scalar.activation(squares[:], o_sb[:], ACT.Square, bias=neg_mean[:], accum_out=ssq[:])
-            sign = work.tile([P, N], F32, name="sign")
-            nc.scalar.activation(sign[:], o_sb[:], ACT.Sign, bias=neg_mean[:])
-            var_eps = stat.tile([P, 1], F32, name="var_eps")
-            nc.gpsimd.tensor_scalar(var_eps[:], ssq[:], 1.0 / N, EPS, op0=ALU.mult, op1=ALU.add)
             rstd = stat.tile([P, 1], F32, name="rstd")
-            nc.gpsimd.tensor_tensor(rstd[:], var_eps[:], neg_half[:], ALU.pow)
+            nc.scalar.activation(rstd[:], ssq[:], ACT.Abs_reciprocal_sqrt, bias=eps[:], scale=1.0 / N)
             shift = stat.tile([P, 1], F32, name="shift")
-            nc.gpsimd.tensor_tensor(shift[:], neg_mean[:], rstd[:], ALU.mult)
+            nc.scalar.activation(shift[:], neg_mean[:], ACT.Identity, scale=rstd[:])
             z = work.tile([P, N], F32, name="z")
             nc.scalar.activation(z[:], o_sb[:], ACT.Identity, bias=shift[:], scale=rstd[:])
             slope = work.tile([P, N], F32, name="slope")
-            nc.gpsimd.tensor_scalar(slope[:], sign[:], 1.0, NEG_SLOPE, op0=ALU.min, op1=ALU.max)
+            nc.vector.tensor_scalar(slope[:], z[:], 0.0, NEG_SLOPE, op0=ALU.is_ge, op1=ALU.max)
             nc.vector.tensor_tensor(window[cb][:].indirect(offsets[:]), z[:], slope[:], ALU.mult)
             nc.sync.dma_start(out_rows[cb], window[cb][:])
 
         waiting = {}
         for jb in range(NB):
-            waiting[jb] = scores(jb)
+            waiting[jb], last_total = scores(jb)
             if jb >= AHEAD:
                 flip_attn(jb - AHEAD, waiting.pop(jb - AHEAD))
-        o_first = acc.tile([P, N], F32, name="o_first", tag="acc")
-        attend(o_first, 0, 0)
+        unused = stat.tile([P, 1], F32, name="unused")
+        nc.scalar.activation(unused[:], last_total[:], ACT.Abs_reciprocal_sqrt)
+        flip_wh(0)
+        o_first = [attend(0, PIECES[0])]
         for jb in range(NB - AHEAD, NB):
             flip_attn(jb, waiting.pop(jb))
-        attend(o_first, 0, 1)
-        place(o_first, 0)
+        o_first += [attend(0, piece) for piece in PIECES[1:]]
         for cb in range(1, CB):
-            o_ps = acc.tile([P, N], F32, name="o_ps", tag="acc")
-            attend(o_ps, cb, 0)
-            attend(o_ps, cb, 1)
-            place(o_ps, cb)
+            flip_wh(cb)
+        place(0, o_first)
+        for cb in range(1, CB):
+            place(cb, [attend(cb, piece) for piece in PIECES])

@@ -100,7 +100,6 @@ def tile_gatconv_b_kernel(tc, base, x, w, offs, out):
         def scores(jb):
             jh, q = divmod(jb, QB)
             sc_ps = [bank("sc_ps0"), bank("sc_ps1")]
-            top2 = stat.tile([P, 2], F32, name="top2")
             for nh in range(2):
                 for cb in range(CB):
                     nc.tensor.matmul(
@@ -110,9 +109,6 @@ def tile_gatconv_b_kernel(tc, base, x, w, offs, out):
                         start=(cb == 0),
                         stop=(cb == CB - 1),
                     )
-                nc.vector.reduce_max(top2[:, nh : nh + 1], sc_ps[nh][:], axis=mybir.AxisListType.X)
-            neg_top = stat.tile([P, 1], F32, name="neg_top")
-            nc.vector.tensor_scalar(neg_top[:], top2[:, 0:1], top2[:, 1:2], -1.0, op0=ALU.max, op1=ALU.mult)
             e_f = soft.tile([P, N], F32, name="e_f")
             sum2 = stat.tile([P, 2], F32, name="sum2")
             for nh in range(2):
@@ -120,7 +116,6 @@ def tile_gatconv_b_kernel(tc, base, x, w, offs, out):
                     e_f[:, nh * HALF : (nh + 1) * HALF],
                     sc_ps[nh][:],
                     ACT.Exp,
-                    bias=neg_top[:],
                     accum_out=sum2[:, nh : nh + 1],
                 )
             total = stat.tile([P, 1], F32, name="total")

@@ -16,6 +16,7 @@ QB = HALF // P
 BIAS = 0.25 + 0.15
 EPS = 1e-5
 NEG_SLOPE = 0.01
+SCALAR_SLOPES_FROM = 2
 AHEAD = 2
 PIECES = ((0, QB), (QB, QB - 1), (NB - 1, 1))
 
@@ -41,7 +42,6 @@ def tile_gatconv_b_kernel(tc, base, x, w, offs, out):
             return banks.tile([P, HALF], F32, name=name, tag="bank")
 
         offsets = held.tile([P, N // 16], U16, name="offsets")
-        nc.sync.dma_start(offsets[:], offs)
         x_bf = [[held.tile([P, HALF], BF16, name=f"x_bf{jh}_{kb}") for kb in range(CB)] for jh in range(2)]
         w_bf = [[held.tile([P, C], BF16, name=f"w_bf{part}_{kb}") for kb in range(CB)] for part in range(2)]
         window = [held.tile([P, S], F32, name=f"window{cb}") for cb in range(CB)]
@@ -55,6 +55,7 @@ def tile_gatconv_b_kernel(tc, base, x, w, offs, out):
         for i, (tile, source) in enumerate(loads):
             queue = nc.sync if i % 2 == 0 else nc.scalar
             queue.dma_start(tile[:], source)
+        nc.sync.dma_start(offsets[:], offs)
 
         ident = held.tile([P, P], BF16, name="ident")
         make_identity(nc, ident[:])
@@ -62,6 +63,8 @@ def tile_gatconv_b_kernel(tc, base, x, w, offs, out):
         nc.vector.memset(tanh_bias[:], BIAS)
         eps = held.tile([P, 1], F32, name="eps")
         nc.vector.memset(eps[:], EPS)
+        mid_slope = held.tile([P, 1], F32, name="mid_slope")
+        nc.vector.memset(mid_slope[:], (1.0 + NEG_SLOPE) / 2)
 
         wh_bf = [[held.tile([P, HALF], BF16, name=f"wh_bf{nh}_{cb}") for cb in range(CB)] for nh in range(2)]
         t_bf = [[held.tile([P, HALF], BF16, name=f"t_bf{jh}_{cb}") for cb in range(CB)] for jh in range(2)]
@@ -168,14 +171,22 @@ def tile_gatconv_b_kernel(tc, base, x, w, offs, out):
             squares = work.tile([P, N], F32, name="squares")
             ssq = stat.tile([P, 1], F32, name="ssq")
             nc.scalar.activation(squares[:], o_sb[:], ACT.Square, bias=neg_mean[:], accum_out=ssq[:])
+            slope = work.tile([P, N], F32, name="slope")
+            if cb < SCALAR_SLOPES_FROM:
+                scaled_up = stat.tile([P, len(PIECES)], F32, name="scaled_up")
+                mean = stat.tile([P, 1], F32, name="mean")
+                nc.scalar.activation(scaled_up[:], osums[:], ACT.Identity, scale=1.0 / N, accum_out=mean[:])
+                nc.vector.tensor_scalar(slope[:], o_sb[:], mean[:], NEG_SLOPE, op0=ALU.is_ge, op1=ALU.max)
             rstd = stat.tile([P, 1], F32, name="rstd")
             nc.scalar.activation(rstd[:], ssq[:], ACT.Abs_reciprocal_sqrt, bias=eps[:], scale=1.0 / N)
             shift = stat.tile([P, 1], F32, name="shift")
             nc.scalar.activation(shift[:], neg_mean[:], ACT.Identity, scale=rstd[:])
             z = work.tile([P, N], F32, name="z")
             nc.scalar.activation(z[:], o_sb[:], ACT.Identity, bias=shift[:], scale=rstd[:])
-            slope = work.tile([P, N], F32, name="slope")
-            nc.vector.tensor_scalar(slope[:], z[:], 0.0, NEG_SLOPE, op0=ALU.is_ge, op1=ALU.max)
+            if cb >= SCALAR_SLOPES_FROM:
+                sign = work.tile([P, N], F32, name="sign")
+                nc.scalar.activation(sign[:], o_sb[:], ACT.Sign, bias=neg_mean[:])
+                nc.scalar.activation(slope[:], sign[:], ACT.Identity, bias=mid_slope[:], scale=(1.0 - NEG_SLOPE) / 2)
             nc.vector.tensor_tensor(window[cb][:].indirect(offsets[:]), z[:], slope[:], ALU.mult)
             nc.sync.dma_start(out_rows[cb], window[cb][:])
 

@@ -16,7 +16,7 @@ QB = HALF // P
 BIAS = 0.25 + 0.15
 EPS = 1e-5
 NEG_SLOPE = 0.01
-SCALAR_SLOPES_FROM = 2
+SCALAR_ALONE_FROM = 2
 AHEAD = 2
 PIECES = ((0, QB), (QB, QB - 1), (NB - 1, 1))
 
@@ -171,19 +171,21 @@ def tile_gatconv_b_kernel(tc, base, x, w, offs, out):
             squares = work.tile([P, N], F32, name="squares")
             ssq = stat.tile([P, 1], F32, name="ssq")
             nc.scalar.activation(squares[:], o_sb[:], ACT.Square, bias=neg_mean[:], accum_out=ssq[:])
+            rstd = stat.tile([P, 1], F32, name="rstd")
+            z = work.tile([P, N], F32, name="z")
             slope = work.tile([P, N], F32, name="slope")
-            if cb < SCALAR_SLOPES_FROM:
+            if cb < SCALAR_ALONE_FROM:
                 scaled_up = stat.tile([P, len(PIECES)], F32, name="scaled_up")
                 mean = stat.tile([P, 1], F32, name="mean")
                 nc.scalar.activation(scaled_up[:], osums[:], ACT.Identity, scale=1.0 / N, accum_out=mean[:])
+                nc.scalar.activation(rstd[:], ssq[:], ACT.Abs_reciprocal_sqrt, bias=eps[:], scale=1.0 / N)
                 nc.vector.tensor_scalar(slope[:], o_sb[:], mean[:], NEG_SLOPE, op0=ALU.is_ge, op1=ALU.max)
-            rstd = stat.tile([P, 1], F32, name="rstd")
-            nc.scalar.activation(rstd[:], ssq[:], ACT.Abs_reciprocal_sqrt, bias=eps[:], scale=1.0 / N)
-            shift = stat.tile([P, 1], F32, name="shift")
-            nc.scalar.activation(shift[:], neg_mean[:], ACT.Identity, scale=rstd[:])
-            z = work.tile([P, N], F32, name="z")
-            nc.scalar.activation(z[:], o_sb[:], ACT.Identity, bias=shift[:], scale=rstd[:])
-            if cb >= SCALAR_SLOPES_FROM:
+                nc.vector.tensor_scalar(z[:], o_sb[:], neg_mean[:], rstd[:], op0=ALU.add, op1=ALU.mult)
+            else:
+                nc.scalar.activation(rstd[:], ssq[:], ACT.Abs_reciprocal_sqrt, bias=eps[:], scale=1.0 / N)
+                shift = stat.tile([P, 1], F32, name="shift")
+                nc.scalar.activation(shift[:], neg_mean[:], ACT.Identity, scale=rstd[:])
+                nc.scalar.activation(z[:], o_sb[:], ACT.Identity, bias=shift[:], scale=rstd[:])
                 sign = work.tile([P, N], F32, name="sign")
                 nc.scalar.activation(sign[:], o_sb[:], ACT.Sign, bias=neg_mean[:])
                 nc.scalar.activation(slope[:], sign[:], ACT.Identity, bias=mid_slope[:], scale=(1.0 - NEG_SLOPE) / 2)

@@ -99,6 +99,8 @@ def tile_gatconv_b_kernel(tc, base, x, w, offs, out):
         for jh in range(2):
             for cb in range(CB):
                 project(jh, cb)
+                if jh == 1 and cb > 0:
+                    flip_wh(cb - 1)
 
         def scores(jb):
             jh, q = divmod(jb, QB)
@@ -195,17 +197,16 @@ def tile_gatconv_b_kernel(tc, base, x, w, offs, out):
         waiting = {}
         for jb in range(NB):
             waiting[jb], last_total = scores(jb)
+            if jb == 0:
+                flip_wh(CB - 1)
             if jb >= AHEAD:
                 flip_attn(jb - AHEAD, waiting.pop(jb - AHEAD))
         unused = stat.tile([P, 1], F32, name="unused")
         nc.scalar.activation(unused[:], last_total[:], ACT.Abs_reciprocal_sqrt)
-        flip_wh(0)
         o_first = [attend(0, PIECES[0])]
         for jb in range(NB - AHEAD, NB):
             flip_attn(jb, waiting.pop(jb))
         o_first += [attend(0, piece) for piece in PIECES[1:]]
-        for cb in range(1, CB):
-            flip_wh(cb)
         place(0, o_first)
         for cb in range(1, CB):
             place(cb, [attend(cb, piece) for piece in PIECES])

@@ -16,7 +16,8 @@ QB = HALF // P
 BIAS = 0.25 + 0.15
 EPS = 1e-5
 NEG_SLOPE = 0.01
-SCALAR_ALONE_FROM = 2
+VECTOR_MAKES_Z_BELOW = 1
+VECTOR_MAKES_SLOPE_BELOW = 2
 AHEAD = 2
 PIECES = ((0, QB), (QB, QB - 1), (NB - 1, 1))
 
@@ -71,7 +72,19 @@ def tile_gatconv_b_kernel(tc, base, x, w, offs, out):
         whT = held.tile([P, NB, C], BF16, name="whT")
         attnT = [held.tile([P, NB, HALF], BF16, name=f"attnT{jh}") for jh in range(2)]
 
-        def project(jh, cb):
+        def flip_start(blocks):
+            flipped_ps = flip.tile([P, NB, P], BF16, name="flipped_ps", tag="flip")
+            return flipped_ps, blocks
+
+        def flip_one(flipping, nb):
+            if flipping is not None:
+                flipped_ps, blocks = flipping
+                nc.tensor.transpose(flipped_ps[:, nb, :], blocks[nb], ident[:])
+
+        def flip_done(flipping, target):
+            nc.vector.tensor_copy(target, flipping[0][:])
+
+        def project(jh, cb, flipping):
             p_ps = [bank("wh_ps"), bank("ws_ps")]
             for part in range(2):
                 for kb in range(CB):
@@ -82,6 +95,7 @@ def tile_gatconv_b_kernel(tc, base, x, w, offs, out):
                         start=(kb == 0),
                         stop=(kb == CB - 1),
                     )
+                    flip_one(flipping, part * CB + kb)
             wh_f = work.tile([P, HALF], F32, name="wh_f")
             nc.scalar.copy(wh_f[:], p_ps[0][:])
             arg = work.tile([P, HALF], F32, name="arg")
@@ -89,20 +103,20 @@ def tile_gatconv_b_kernel(tc, base, x, w, offs, out):
             nc.vector.tensor_copy(wh_bf[jh][cb][:], wh_f[:])
             nc.scalar.activation(t_bf[jh][cb][:], arg[:], ACT.Tanh, bias=tanh_bias[:])
 
-        def flip_wh(cb):
-            whT_ps = flip.tile([P, NB, P], BF16, name="whT_ps", tag="flip")
-            for nb in range(NB):
-                nh, q = divmod(nb, QB)
-                nc.tensor.transpose(whT_ps[:, nb, :], wh_bf[nh][cb][:, q * P : (q + 1) * P], ident[:])
-            nc.vector.tensor_copy(whT[:, :, cb * P : (cb + 1) * P], whT_ps[:])
+        def wh_blocks(cb):
+            return [wh_bf[nb // QB][cb][:, (nb % QB) * P : (nb % QB + 1) * P] for nb in range(NB)]
+
+        def whT_block(cb):
+            return whT[:, :, cb * P : (cb + 1) * P]
 
         for jh in range(2):
             for cb in range(CB):
-                project(jh, cb)
-                if jh == 1 and cb > 0:
-                    flip_wh(cb - 1)
+                flipping = flip_start(wh_blocks(cb - 1)) if jh == 1 and cb > 0 else None
+                project(jh, cb, flipping)
+                if flipping is not None:
+                    flip_done(flipping, whT_block(cb - 1))
 
-        def scores(jb):
+        def scores(jb, flipping):
             jh, q = divmod(jb, QB)
             sc_ps = [bank("sc_ps0"), bank("sc_ps1")]
             for nh in range(2):
@@ -114,6 +128,7 @@ def tile_gatconv_b_kernel(tc, base, x, w, offs, out):
                         start=(cb == 0),
                         stop=(cb == CB - 1),
                     )
+                    flip_one(flipping, nh * CB + cb)
             e_f = soft.tile([P, N], F32, name="e_f")
             sum2 = stat.tile([P, 2], F32, name="sum2")
             for nh in range(2):
@@ -131,17 +146,7 @@ def tile_gatconv_b_kernel(tc, base, x, w, offs, out):
             nc.vector.tensor_scalar(attn_bf[:], e_f[:], rinv[:], None, op0=ALU.mult)
             return attn_bf, total
 
-        def flip_attn(jb, attn_bf):
-            jh, q = divmod(jb, QB)
-            aT_ps = flip.tile([P, NB, P], BF16, name="aT_ps", tag="flip")
-            for nb in range(NB):
-                nc.tensor.transpose(aT_ps[:, nb, :], attn_bf[:, nb * P : (nb + 1) * P], ident[:])
-            if jb % 2 == 0:
-                nc.scalar.copy(attnT[jh][:, :, q * P : (q + 1) * P], aT_ps[:])
-            else:
-                nc.vector.tensor_copy(attnT[jh][:, :, q * P : (q + 1) * P], aT_ps[:])
-
-        def attend(cb, piece):
+        def attend(cb, piece, flipping=None):
             first_jb, blocks = piece
             jh, q = divmod(first_jb, QB)
             in_half = slice(q * P, (q + blocks) * P)
@@ -154,6 +159,7 @@ def tile_gatconv_b_kernel(tc, base, x, w, offs, out):
                     start=(nb == 0),
                     stop=False,
                 )
+                flip_one(flipping, nb)
             nc.tensor.matmul(o_ps[:, 0 : blocks * P], lhsT=ident[:], rhs=x_bf[jh][cb][:, in_half], start=False, stop=True)
             return o_ps
 
@@ -173,40 +179,54 @@ def tile_gatconv_b_kernel(tc, base, x, w, offs, out):
             squares = work.tile([P, N], F32, name="squares")
             ssq = stat.tile([P, 1], F32, name="ssq")
             nc.scalar.activation(squares[:], o_sb[:], ACT.Square, bias=neg_mean[:], accum_out=ssq[:])
-            rstd = stat.tile([P, 1], F32, name="rstd")
-            z = work.tile([P, N], F32, name="z")
             slope = work.tile([P, N], F32, name="slope")
-            if cb < SCALAR_ALONE_FROM:
+            if cb < VECTOR_MAKES_SLOPE_BELOW:
                 scaled_up = stat.tile([P, len(PIECES)], F32, name="scaled_up")
                 mean = stat.tile([P, 1], F32, name="mean")
                 nc.scalar.activation(scaled_up[:], osums[:], ACT.Identity, scale=1.0 / N, accum_out=mean[:])
-                nc.scalar.activation(rstd[:], ssq[:], ACT.Abs_reciprocal_sqrt, bias=eps[:], scale=1.0 / N)
                 nc.vector.tensor_scalar(slope[:], o_sb[:], mean[:], NEG_SLOPE, op0=ALU.is_ge, op1=ALU.max)
+            rstd = stat.tile([P, 1], F32, name="rstd")
+            nc.scalar.activation(rstd[:], ssq[:], ACT.Abs_reciprocal_sqrt, bias=eps[:], scale=1.0 / N)
+            z = work.tile([P, N], F32, name="z")
+            if cb < VECTOR_MAKES_Z_BELOW:
                 nc.vector.tensor_scalar(z[:], o_sb[:], neg_mean[:], rstd[:], op0=ALU.add, op1=ALU.mult)
             else:
-                nc.scalar.activation(rstd[:], ssq[:], ACT.Abs_reciprocal_sqrt, bias=eps[:], scale=1.0 / N)
                 shift = stat.tile([P, 1], F32, name="shift")
                 nc.scalar.activation(shift[:], neg_mean[:], ACT.Identity, scale=rstd[:])
                 nc.scalar.activation(z[:], o_sb[:], ACT.Identity, bias=shift[:], scale=rstd[:])
+            if cb >= VECTOR_MAKES_SLOPE_BELOW:
                 sign = work.tile([P, N], F32, name="sign")
                 nc.scalar.activation(sign[:], o_sb[:], ACT.Sign, bias=neg_mean[:])
                 nc.scalar.activation(slope[:], sign[:], ACT.Identity, bias=mid_slope[:], scale=(1.0 - NEG_SLOPE) / 2)
             nc.vector.tensor_tensor(window[cb][:].indirect(offsets[:]), z[:], slope[:], ALU.mult)
             nc.sync.dma_start(out_rows[cb], window[cb][:])
 
+        def attn_blocks(attn_bf):
+            return [attn_bf[:, nb * P : (nb + 1) * P] for nb in range(NB)]
+
+        def attnT_block(jb):
+            return attnT[jb // QB][:, :, (jb % QB) * P : (jb % QB + 1) * P]
+
         waiting = {}
         for jb in range(NB):
-            waiting[jb], last_total = scores(jb)
             if jb == 0:
-                flip_wh(CB - 1)
-            if jb >= AHEAD:
-                flip_attn(jb - AHEAD, waiting.pop(jb - AHEAD))
+                flipping, target = flip_start(wh_blocks(CB - 1)), whT_block(CB - 1)
+            elif jb >= AHEAD:
+                flipping, target = flip_start(attn_blocks(waiting.pop(jb - AHEAD))), attnT_block(jb - AHEAD)
+            else:
+                flipping = None
+            waiting[jb], last_total = scores(jb, flipping)
+            if flipping is not None:
+                flip_done(flipping, target)
         unused = stat.tile([P, 1], F32, name="unused")
         nc.scalar.activation(unused[:], last_total[:], ACT.Abs_reciprocal_sqrt)
-        o_first = [attend(0, PIECES[0])]
-        for jb in range(NB - AHEAD, NB):
-            flip_attn(jb, waiting.pop(jb))
-        o_first += [attend(0, piece) for piece in PIECES[1:]]
+        o_first = []
+        for i, piece in enumerate(PIECES):
+            jb = NB - AHEAD + i
+            flipping = flip_start(attn_blocks(waiting.pop(jb))) if jb < NB else None
+            o_first.append(attend(0, piece, flipping))
+            if flipping is not None:
+                flip_done(flipping, attnT_block(jb))
         place(0, o_first)
         for cb in range(1, CB):
             place(cb, [attend(cb, piece) for piece in PIECES])

@@ -72,14 +72,18 @@ def tile_gatconv_b_kernel(tc, base, x, w, offs, out):
         whT = held.tile([P, NB, C], BF16, name="whT")
         attnT = [held.tile([P, NB, HALF], BF16, name=f"attnT{jh}") for jh in range(2)]
 
-        def flip_start(blocks):
-            flipped_ps = flip.tile([P, NB, P], BF16, name="flipped_ps", tag="flip")
-            return flipped_ps, blocks
+        EARLY, LATE = 0, NB // 2
 
-        def flip_one(flipping, nb):
+        def flip_start(blocks, first_step):
+            flipped_ps = flip.tile([P, NB, P], BF16, name="flipped_ps", tag="flip")
+            return flipped_ps, blocks, first_step
+
+        def flip_one(flipping, step):
             if flipping is not None:
-                flipped_ps, blocks = flipping
-                nc.tensor.transpose(flipped_ps[:, nb, :], blocks[nb], ident[:])
+                flipped_ps, blocks, first_step = flipping
+                if first_step <= step < first_step + NB // 2:
+                    for nb in range(2 * (step - first_step), 2 * (step - first_step) + 2):
+                        nc.tensor.transpose(flipped_ps[:, nb, :], blocks[nb], ident[:])
 
         def flip_done(flipping, target):
             nc.vector.tensor_copy(target, flipping[0][:])
@@ -111,7 +115,7 @@ def tile_gatconv_b_kernel(tc, base, x, w, offs, out):
 
         for jh in range(2):
             for cb in range(CB):
-                flipping = flip_start(wh_blocks(cb - 1)) if jh == 1 and cb > 0 else None
+                flipping = flip_start(wh_blocks(cb - 1), LATE) if jh == 1 and cb > 0 else None
                 project(jh, cb, flipping)
                 if flipping is not None:
                     flip_done(flipping, whT_block(cb - 1))
@@ -210,9 +214,9 @@ def tile_gatconv_b_kernel(tc, base, x, w, offs, out):
         waiting = {}
         for jb in range(NB):
             if jb == 0:
-                flipping, target = flip_start(wh_blocks(CB - 1)), whT_block(CB - 1)
+                flipping, target = flip_start(wh_blocks(CB - 1), LATE), whT_block(CB - 1)
             elif jb >= AHEAD:
-                flipping, target = flip_start(attn_blocks(waiting.pop(jb - AHEAD))), attnT_block(jb - AHEAD)
+                flipping, target = flip_start(attn_blocks(waiting.pop(jb - AHEAD)), LATE), attnT_block(jb - AHEAD)
             else:
                 flipping = None
             waiting[jb], last_total = scores(jb, flipping)
@@ -223,7 +227,7 @@ def tile_gatconv_b_kernel(tc, base, x, w, offs, out):
         o_first = []
         for i, piece in enumerate(PIECES):
             jb = NB - AHEAD + i
-            flipping = flip_start(attn_blocks(waiting.pop(jb))) if jb < NB else None
+            flipping = flip_start(attn_blocks(waiting.pop(jb)), EARLY) if jb < NB else None
             o_first.append(attend(0, piece, flipping))
             if flipping is not None:
                 flip_done(flipping, attnT_block(jb))

@@ -227,7 +227,7 @@ def tile_gatconv_b_kernel(tc, base, x, w, offs, out):
         o_first = []
         for i, piece in enumerate(PIECES):
             jb = NB - AHEAD + i
-            flipping = flip_start(attn_blocks(waiting.pop(jb)), EARLY) if jb < NB else None
+            flipping = flip_start(attn_blocks(waiting.pop(jb)), (2, EARLY)[i]) if jb < NB else None
             o_first.append(attend(0, piece, flipping))
             if flipping is not None:
                 flip_done(flipping, attnT_block(jb))

@@ -16,10 +16,10 @@ QB = HALF // P
 BIAS = 0.25 + 0.15
 EPS = 1e-5
 NEG_SLOPE = 0.01
-VECTOR_MAKES_Z_BELOW = 1
 VECTOR_MAKES_SLOPE_BELOW = 2
 AHEAD = 2
 PIECES = ((0, QB), (QB, QB - 1), (NB - 1, 1))
+FIRST_PIECES = ((0, QB), (QB, QB - AHEAD), (NB - 2, 1), (NB - 1, 1))
 
 FLOPS = 3 * 2 * C * N * N
 
@@ -167,16 +167,37 @@ def tile_gatconv_b_kernel(tc, base, x, w, offs, out):
             nc.tensor.matmul(o_ps[:, 0 : blocks * P], lhsT=ident[:], rhs=x_bf[jh][cb][:, in_half], start=False, stop=True)
             return o_ps
 
+        def place_first(o_sb, pieces):
+            stats = stat.tile([P, len(FIRST_PIECES), 6], F32, name="stats")
+            for i, (target, source) in enumerate(pieces):
+                nc.vector.bn_stats(stats[:, i, :], source)
+                if i < len(FIRST_PIECES) - 1:
+                    nc.scalar.copy(target, source)
+                else:
+                    nc.vector.tensor_copy(target, source)
+            mean_var = stat.tile([P, 2], F32, name="mean_var")
+            nc.vector.bn_aggr(mean_var[:], stats[:])
+            rstd = stat.tile([P, 1], F32, name="rstd0")
+            nc.scalar.activation(rstd[:], mean_var[:, 1:2], ACT.Abs_reciprocal_sqrt, bias=eps[:])
+            slope = work.tile([P, N], F32, name="slope")
+            nc.vector.tensor_scalar(slope[:], o_sb[:], mean_var[:, 0:1], NEG_SLOPE, op0=ALU.is_ge, op1=ALU.max)
+            z = work.tile([P, N], F32, name="z")
+            nc.vector.tensor_scalar(z[:], o_sb[:], mean_var[:, 0:1], rstd[:], op0=ALU.subtract, op1=ALU.mult)
+            nc.vector.tensor_tensor(window[0][:].indirect(offsets[:]), z[:], slope[:], ALU.mult)
+            nc.sync.dma_start(out_rows[0], window[0][:])
+
         def place(cb, o_pieces):
             o_sb = work.tile([P, N], F32, name="o_sb")
+            pieces = [
+                (o_sb[:, first_jb * P : (first_jb + blocks) * P], o_ps[:, 0 : blocks * P])
+                for (first_jb, blocks), o_ps in zip(FIRST_PIECES if cb == 0 else PIECES, o_pieces)
+            ]
+            if cb == 0:
+                place_first(o_sb, pieces)
+                return
             osums = stat.tile([P, len(PIECES)], F32, name="osums")
-            for i, (first_jb, blocks) in enumerate(PIECES):
-                nc.scalar.activation(
-                    o_sb[:, first_jb * P : (first_jb + blocks) * P],
-                    o_pieces[i][:, 0 : blocks * P],
-                    ACT.Identity,
-                    accum_out=osums[:, i : i + 1],
-                )
+            for i, (target, source) in enumerate(pieces):
+                nc.scalar.activation(target, source, ACT.Identity, accum_out=osums[:, i : i + 1])
             scaled = stat.tile([P, len(PIECES)], F32, name="scaled")
             neg_mean = stat.tile([P, 1], F32, name="neg_mean")
             nc.scalar.activation(scaled[:], osums[:], ACT.Identity, scale=-1.0 / N, accum_out=neg_mean[:])
@@ -192,12 +213,9 @@ def tile_gatconv_b_kernel(tc, base, x, w, offs, out):
             rstd = stat.tile([P, 1], F32, name="rstd")
             nc.scalar.activation(rstd[:], ssq[:], ACT.Abs_reciprocal_sqrt, bias=eps[:], scale=1.0 / N)
             z = work.tile([P, N], F32, name="z")
-            if cb < VECTOR_MAKES_Z_BELOW:
-                nc.vector.tensor_scalar(z[:], o_sb[:], neg_mean[:], rstd[:], op0=ALU.add, op1=ALU.mult)
-            else:
-                shift = stat.tile([P, 1], F32, name="shift")
-                nc.scalar.activation(shift[:], neg_mean[:], ACT.Identity, scale=rstd[:])
-                nc.scalar.activation(z[:], o_sb[:], ACT.Identity, bias=shift[:], scale=rstd[:])
+            shift = stat.tile([P, 1], F32, name="shift")
+            nc.scalar.activation(shift[:], neg_mean[:], ACT.Identity, scale=rstd[:])
+            nc.scalar.activation(z[:], o_sb[:], ACT.Identity, bias=shift[:], scale=rstd[:])
             if cb >= VECTOR_MAKES_SLOPE_BELOW:
                 sign = work.tile([P, N], F32, name="sign")
                 nc.scalar.activation(sign[:], o_sb[:], ACT.Sign, bias=neg_mean[:])
@@ -225,9 +243,9 @@ def tile_gatconv_b_kernel(tc, base, x, w, offs, out):
         unused = stat.tile([P, 1], F32, name="unused")
         nc.scalar.activation(unused[:], last_total[:], ACT.Abs_reciprocal_sqrt)
         o_first = []
-        for i, piece in enumerate(PIECES):
+        for i, piece in enumerate(FIRST_PIECES):
             jb = NB - AHEAD + i
-            flipping = flip_start(attn_blocks(waiting.pop(jb)), (2, EARLY)[i]) if jb < NB else None
+            flipping = flip_start(attn_blocks(waiting.pop(jb)), EARLY) if jb < NB else None
             o_first.append(attend(0, piece, flipping))
             if flipping is not None:
                 flip_done(flipping, attnT_block(jb))

@@ -48,14 +48,15 @@ def tile_gatconv_b_kernel(tc, base, x, w, offs, out):
         window = [held.tile([P, S], F32, name=f"window{cb}") for cb in range(CB)]
         loads = []
         for kb in range(CB):
-            loads.append((x_bf[0][kb], x_rows[kb][:, 0:HALF]))
-            loads.append((w_bf[0][kb], w_rows[kb][:, 0:C]))
-        loads += [(w_bf[1][kb], w_rows[kb][:, C : 2 * C]) for kb in range(CB)]
-        loads += [(x_bf[1][kb], x_rows[kb][:, HALF:N]) for kb in range(CB)]
-        loads += [(window[cb], base_rows[cb]) for cb in range(CB)]
-        for i, (tile, source) in enumerate(loads):
+            loads.append((w_bf[0][kb][:, 0:P], w_rows[kb][:, 0:P]))
+            loads.append((x_bf[0][kb][:], x_rows[kb][:, 0:HALF]))
+        loads += [(w_bf[1][kb][:], w_rows[kb][:, C : 2 * C]) for kb in range(CB)]
+        loads += [(w_bf[0][kb][:, P:C], w_rows[kb][:, P:C]) for kb in range(CB)]
+        loads += [(x_bf[1][kb][:], x_rows[kb][:, HALF:N]) for kb in range(CB)]
+        loads += [(window[cb][:], base_rows[cb]) for cb in range(CB)]
+        for i, (target, source) in enumerate(loads):
             queue = nc.sync if i % 2 == 0 else nc.scalar
-            queue.dma_start(tile[:], source)
+            queue.dma_start(target, source)
         nc.sync.dma_start(offsets[:], offs)
 
         ident = held.tile([P, P], BF16, name="ident")

@@ -148,7 +148,8 @@ def tile_gatconv_b_kernel(tc, base, x, w, offs, out):
             rinv = stat.tile([P, 1], F32, name="rinv")
             nc.vector.reciprocal(rinv[:], total[:])
             attn_bf = soft.tile([P, N], BF16, name="attn_bf")
-            nc.vector.tensor_scalar(attn_bf[:], e_f[:], rinv[:], None, op0=ALU.mult)
+            for half in (slice(0, HALF), slice(HALF, N)):
+                nc.vector.tensor_scalar(attn_bf[:, half], e_f[:, half], rinv[:], None, op0=ALU.mult)
             return attn_bf, total
 
         def attend(cb, piece, flipping=None):
@@ -246,7 +247,7 @@ def tile_gatconv_b_kernel(tc, base, x, w, offs, out):
         o_first = []
         for i, piece in enumerate(FIRST_PIECES):
             jb = NB - AHEAD + i
-            flipping = flip_start(attn_blocks(waiting.pop(jb)), EARLY) if jb < NB else None
+            flipping = flip_start(attn_blocks(waiting.pop(jb)), (LATE, EARLY)[i]) if jb < NB else None
             o_first.append(attend(0, piece, flipping))
             if flipping is not None:
                 flip_done(flipping, attnT_block(jb))

@@ -17,6 +17,7 @@ BIAS = 0.25 + 0.15
 EPS = 1e-5
 NEG_SLOPE = 0.01
 VECTOR_MAKES_SLOPE_BELOW = 2
+FIRST_BLOCK_PARTS = (slice(0, 3 * P), slice(3 * P, N))
 AHEAD = 2
 PIECES = ((0, QB), (QB, QB - 1), (NB - 1, 1))
 FIRST_PIECES = ((0, QB), (QB, QB - AHEAD), (NB - 2, 1), (NB - 1, 1))
@@ -169,6 +170,18 @@ def tile_gatconv_b_kernel(tc, base, x, w, offs, out):
             nc.tensor.matmul(o_ps[:, 0 : blocks * P], lhsT=ident[:], rhs=x_bf[jh][cb][:, in_half], start=False, stop=True)
             return o_ps
 
+        def make_slope(slope, o_sb, neg_mean, nodes):
+            sign = work.tile([P, N], F32, name="sign")
+            nc.scalar.activation(sign[:, nodes], o_sb[:, nodes], ACT.Sign, bias=neg_mean[:])
+            nc.scalar.activation(
+                slope[:, nodes], sign[:, nodes], ACT.Identity, bias=mid_slope[:], scale=(1.0 - NEG_SLOPE) / 2
+            )
+
+        def make_z(z, o_sb, neg_mean, rstd, nodes):
+            shift = stat.tile([P, 1], F32, name="shift")
+            nc.scalar.activation(shift[:], neg_mean[:], ACT.Identity, scale=rstd[:])
+            nc.scalar.activation(z[:, nodes], o_sb[:, nodes], ACT.Identity, bias=shift[:], scale=rstd[:])
+
         def place_first(o_sb, pieces):
             stats = stat.tile([P, len(FIRST_PIECES), 6], F32, name="stats")
             for i, (target, source) in enumerate(pieces):
@@ -182,10 +195,21 @@ def tile_gatconv_b_kernel(tc, base, x, w, offs, out):
             rstd = stat.tile([P, 1], F32, name="rstd0")
             nc.scalar.activation(rstd[:], mean_var[:, 1:2], ACT.Abs_reciprocal_sqrt, bias=eps[:])
             slope = work.tile([P, N], F32, name="slope")
-            nc.vector.tensor_scalar(slope[:], o_sb[:], mean_var[:, 0:1], NEG_SLOPE, op0=ALU.is_ge, op1=ALU.max)
             z = work.tile([P, N], F32, name="z")
-            nc.vector.tensor_scalar(z[:], o_sb[:], mean_var[:, 0:1], rstd[:], op0=ALU.subtract, op1=ALU.mult)
-            nc.vector.tensor_tensor(window[0][:].indirect(offsets[:]), z[:], slope[:], ALU.mult)
+            first, second = FIRST_BLOCK_PARTS
+            nc.vector.tensor_scalar(
+                slope[:, first], o_sb[:, first], mean_var[:, 0:1], NEG_SLOPE, op0=ALU.is_ge, op1=ALU.max
+            )
+            nc.vector.tensor_scalar(
+                z[:, first], o_sb[:, first], mean_var[:, 0:1], rstd[:], op0=ALU.subtract, op1=ALU.mult
+            )
+            neg_mean = stat.tile([P, 1], F32, name="neg_mean0")
+            nc.scalar.mul(neg_mean[:], mean_var[:, 0:1], -1.0)
+            make_slope(slope, o_sb, neg_mean, second)
+            make_z(z, o_sb, neg_mean, rstd, second)
+            for nodes in FIRST_BLOCK_PARTS:
+                entries = offsets[:, nodes.start // 16 : nodes.stop // 16]
+                nc.vector.tensor_tensor(window[0][:].indirect(entries), z[:, nodes], slope[:, nodes], ALU.mult)
             nc.sync.dma_start(out_rows[0], window[0][:])
 
         def place(cb, o_pieces):
@@ -215,13 +239,9 @@ def tile_gatconv_b_kernel(tc, base, x, w, offs, out):
             rstd = stat.tile([P, 1], F32, name="rstd")
             nc.scalar.activation(rstd[:], ssq[:], ACT.Abs_reciprocal_sqrt, bias=eps[:], scale=1.0 / N)
             z = work.tile([P, N], F32, name="z")
-            shift = stat.tile([P, 1], F32, name="shift")
-            nc.scalar.activation(shift[:], neg_mean[:], ACT.Identity, scale=rstd[:])
-            nc.scalar.activation(z[:], o_sb[:], ACT.Identity, bias=shift[:], scale=rstd[:])
+            make_z(z, o_sb, neg_mean, rstd, slice(0, N))
             if cb >= VECTOR_MAKES_SLOPE_BELOW:
-                sign = work.tile([P, N], F32, name="sign")
-                nc.scalar.activation(sign[:], o_sb[:], ACT.Sign, bias=neg_mean[:])
-                nc.scalar.activation(slope[:], sign[:], ACT.Identity, bias=mid_slope[:], scale=(1.0 - NEG_SLOPE) / 2)
+                make_slope(slope, o_sb, neg_mean, slice(0, N))
             nc.vector.tensor_tensor(window[cb][:].indirect(offsets[:]), z[:], slope[:], ALU.mult)
             nc.sync.dma_start(out_rows[cb], window[cb][:])
 

import concourse.mybir as mybir
from concourse.masks import make_identity

BF16, F32, U16 = mybir.dt.bfloat16, mybir.dt.float32, mybir.dt.uint16
ALU = mybir.AluOpType
ACT = mybir.ActivationFunctionType

P = 128
C = 512
N = 1024
S = 2048
CB = C // P
NB = N // P
HALF = 512
QB = HALF // P
BIAS = 0.25 + 0.15
EPS = 1e-5
NEG_SLOPE = 0.01
VECTOR_MAKES_SLOPE_BELOW = 2
FIRST_BLOCK_PARTS = (slice(0, 3 * P), slice(3 * P, N))
AHEAD = 2
PIECES = ((0, QB), (QB, QB - 1), (NB - 1, 1))
FIRST_PIECES = ((0, QB), (QB, QB - AHEAD), (NB - 2, 1), (NB - 1, 1))

FLOPS = 3 * 2 * C * N * N


def tile_gatconv_b_kernel(tc, base, x, w, offs, out):
    nc = tc.nc
    base_rows = base.rearrange("(cb p) s -> cb p s", p=P)
    out_rows = out.rearrange("(cb p) s -> cb p s", p=P)
    x_rows = x.rearrange("(kb p) j -> kb p j", p=P)
    w_rows = w.rearrange("(kb p) m -> kb p m", p=P)

    with (
        tc.tile_pool(name="held", bufs=1) as held,
        tc.tile_pool(name="work", bufs=2) as work,
        tc.tile_pool(name="soft", bufs=AHEAD + 1) as soft,
        tc.tile_pool(name="stat", bufs=4) as stat,
        tc.psum_pool(name="banks", bufs=6) as banks,
        tc.psum_pool(name="flip", bufs=2) as flip,
    ):
        def bank(name):
            return banks.tile([P, HALF], F32, name=name, tag="bank")

        offsets = held.tile([P, N // 16], U16, name="offsets")
        x_bf = [[held.tile([P, HALF], BF16, name=f"x_bf{jh}_{kb}") for kb in range(CB)] for jh in range(2)]
        w_bf = [[held.tile([P, C], BF16, name=f"w_bf{part}_{kb}") for kb in range(CB)] for part in range(2)]
        window = [held.tile([P, S], F32, name=f"window{cb}") for cb in range(CB)]
        loads = []
        for kb in range(CB):
            loads.append((w_bf[0][kb][:, 0:P], w_rows[kb][:, 0:P]))
            loads.append((x_bf[0][kb][:], x_rows[kb][:, 0:HALF]))
        loads += [(w_bf[1][kb][:], w_rows[kb][:, C : 2 * C]) for kb in range(CB)]
        loads += [(w_bf[0][kb][:, P:C], w_rows[kb][:, P:C]) for kb in range(CB)]
        loads += [(x_bf[1][kb][:], x_rows[kb][:, HALF:N]) for kb in range(CB)]
        loads += [(window[cb][:], base_rows[cb]) for cb in range(CB)]
        for i, (target, source) in enumerate(loads):
            queue = nc.sync if i % 2 == 0 else nc.scalar
            queue.dma_start(target, source)
        nc.sync.dma_start(offsets[:], offs)

        ident = held.tile([P, P], BF16, name="ident")
        make_identity(nc, ident[:])
        tanh_bias = held.tile([P, 1], F32, name="tanh_bias")
        nc.vector.memset(tanh_bias[:], BIAS)
        eps = held.tile([P, 1], F32, name="eps")
        nc.vector.memset(eps[:], EPS)
        mid_slope = held.tile([P, 1], F32, name="mid_slope")
        nc.vector.memset(mid_slope[:], (1.0 + NEG_SLOPE) / 2)

        wh_bf = [[held.tile([P, HALF], BF16, name=f"wh_bf{nh}_{cb}") for cb in range(CB)] for nh in range(2)]
        t_bf = [[held.tile([P, HALF], BF16, name=f"t_bf{jh}_{cb}") for cb in range(CB)] for jh in range(2)]
        whT = held.tile([P, NB, C], BF16, name="whT")
        attnT = [held.tile([P, NB, HALF], BF16, name=f"attnT{jh}") for jh in range(2)]

        EARLY, LATE = 0, NB // 2

        def flip_start(blocks, first_step):
            flipped_ps = flip.tile([P, NB, P], BF16, name="flipped_ps", tag="flip")
            return flipped_ps, blocks, first_step

        def flip_one(flipping, step):
            if flipping is not None:
                flipped_ps, blocks, first_step = flipping
                if first_step <= step < first_step + NB // 2:
                    for nb in range(2 * (step - first_step), 2 * (step - first_step) + 2):
                        nc.tensor.transpose(flipped_ps[:, nb, :], blocks[nb], ident[:])

        def flip_done(flipping, target):
            nc.vector.tensor_copy(target, flipping[0][:])

        def project(jh, cb, flipping):
            p_ps = [bank("wh_ps"), bank("ws_ps")]
            for part in range(2):
                for kb in range(CB):
                    nc.tensor.matmul(
                        p_ps[part][:],
                        lhsT=w_bf[part][kb][:, cb * P : (cb + 1) * P],
                        rhs=x_bf[jh][kb][:],
                        start=(kb == 0),
                        stop=(kb == CB - 1),
                    )
                    flip_one(flipping, part * CB + kb)
            wh_f = work.tile([P, HALF], F32, name="wh_f")
            nc.scalar.copy(wh_f[:], p_ps[0][:])
            arg = work.tile([P, HALF], F32, name="arg")
            nc.vector.tensor_tensor(arg[:], p_ps[1][:], wh_f[:], ALU.add)
            nc.vector.tensor_copy(wh_bf[jh][cb][:], wh_f[:])
            nc.scalar.activation(t_bf[jh][cb][:], arg[:], ACT.Tanh, bias=tanh_bias[:])

        def wh_blocks(cb):
            return [wh_bf[nb // QB][cb][:, (nb % QB) * P : (nb % QB + 1) * P] for nb in range(NB)]

        def whT_block(cb):
            return whT[:, :, cb * P : (cb + 1) * P]

        for jh in range(2):
            for cb in range(CB):
                flipping = flip_start(wh_blocks(cb - 1), LATE) if jh == 1 and cb > 0 else None
                project(jh, cb, flipping)
                if flipping is not None:
                    flip_done(flipping, whT_block(cb - 1))

        def scores(jb, flipping):
            jh, q = divmod(jb, QB)
            sc_ps = [bank("sc_ps0"), bank("sc_ps1")]
            for nh in range(2):
                for cb in range(CB):
                    nc.tensor.matmul(
                        sc_ps[nh][:],
                        lhsT=t_bf[jh][cb][:, q * P : (q + 1) * P],
                        rhs=wh_bf[nh][cb][:],
                        start=(cb == 0),
                        stop=(cb == CB - 1),
                    )
                    flip_one(flipping, nh * CB + cb)
            e_f = soft.tile([P, N], F32, name="e_f")
            sum2 = stat.tile([P, 2], F32, name="sum2")
            for nh in range(2):
                nc.scalar.activation(
                    e_f[:, nh * HALF : (nh + 1) * HALF],
                    sc_ps[nh][:],
                    ACT.Exp,
                    accum_out=sum2[:, nh : nh + 1],
                )
            total = stat.tile([P, 1], F32, name="total")
            nc.vector.tensor_tensor(total[:], sum2[:, 0:1], sum2[:, 1:2], ALU.add)
            rinv = stat.tile([P, 1], F32, name="rinv")
            nc.vector.reciprocal(rinv[:], total[:])
            attn_bf = soft.tile([P, N], BF16, name="attn_bf")
            for half in (slice(0, HALF), slice(HALF, N)):
                nc.vector.tensor_scalar(attn_bf[:, half], e_f[:, half], rinv[:], None, op0=ALU.mult)
            return attn_bf, total

        def attend(cb, piece, flipping=None):
            first_jb, blocks = piece
            jh, q = divmod(first_jb, QB)
            in_half = slice(q * P, (q + blocks) * P)
            o_ps = bank("o_ps")
            for nb in range(NB):
                nc.tensor.matmul(
                    o_ps[:, 0 : blocks * P],
                    lhsT=whT[:, nb, cb * P : (cb + 1) * P],
                    rhs=attnT[jh][:, nb, in_half],
                    start=(nb == 0),
                    stop=False,
                )
                flip_one(flipping, nb)
            nc.tensor.matmul(o_ps[:, 0 : blocks * P], lhsT=ident[:], rhs=x_bf[jh][cb][:, in_half], start=False, stop=True)
            return o_ps

        def make_slope(slope, o_sb, neg_mean, nodes):
            sign = work.tile([P, N], F32, name="sign")
            nc.scalar.activation(sign[:, nodes], o_sb[:, nodes], ACT.Sign, bias=neg_mean[:])
            nc.scalar.activation(
                slope[:, nodes], sign[:, nodes], ACT.Identity, bias=mid_slope[:], scale=(1.0 - NEG_SLOPE) / 2
            )

        def make_z(z, o_sb, neg_mean, rstd, nodes):
            shift = stat.tile([P, 1], F32, name="shift")
            nc.scalar.activation(shift[:], neg_mean[:], ACT.Identity, scale=rstd[:])
            nc.scalar.activation(z[:, nodes], o_sb[:, nodes], ACT.Identity, bias=shift[:], scale=rstd[:])

        def place_first(o_sb, pieces):
            stats = stat.tile([P, len(FIRST_PIECES), 6], F32, name="stats")
            for i, (target, source) in enumerate(pieces):
                nc.vector.bn_stats(stats[:, i, :], source)
                if i < len(FIRST_PIECES) - 1:
                    nc.scalar.copy(target, source)
                else:
                    nc.vector.tensor_copy(target, source)
            mean_var = stat.tile([P, 2], F32, name="mean_var")
            nc.vector.bn_aggr(mean_var[:], stats[:])
            rstd = stat.tile([P, 1], F32, name="rstd0")
            nc.scalar.activation(rstd[:], mean_var[:, 1:2], ACT.Abs_reciprocal_sqrt, bias=eps[:])
            slope = work.tile([P, N], F32, name="slope")
            z = work.tile([P, N], F32, name="z")
            first, second = FIRST_BLOCK_PARTS
            nc.vector.tensor_scalar(
                slope[:, first], o_sb[:, first], mean_var[:, 0:1], NEG_SLOPE, op0=ALU.is_ge, op1=ALU.max
            )
            nc.vector.tensor_scalar(
                z[:, first], o_sb[:, first], mean_var[:, 0:1], rstd[:], op0=ALU.subtract, op1=ALU.mult
            )
            neg_mean = stat.tile([P, 1], F32, name="neg_mean0")
            nc.scalar.mul(neg_mean[:], mean_var[:, 0:1], -1.0)
            make_slope(slope, o_sb, neg_mean, second)
            make_z(z, o_sb, neg_mean, rstd, second)
            for nodes in FIRST_BLOCK_PARTS:
                entries = offsets[:, nodes.start // 16 : nodes.stop // 16]
                nc.vector.tensor_tensor(window[0][:].indirect(entries), z[:, nodes], slope[:, nodes], ALU.mult)
            nc.sync.dma_start(out_rows[0], window[0][:])

        def place(cb, o_pieces):
            o_sb = work.tile([P, N], F32, name="o_sb")
            pieces = [
                (o_sb[:, first_jb * P : (first_jb + blocks) * P], o_ps[:, 0 : blocks * P])
                for (first_jb, blocks), o_ps in zip(FIRST_PIECES if cb == 0 else PIECES, o_pieces)
            ]
            if cb == 0:
                place_first(o_sb, pieces)
                return
            osums = stat.tile([P, len(PIECES)], F32, name="osums")
            for i, (target, source) in enumerate(pieces):
                nc.scalar.activation(target, source, ACT.Identity, accum_out=osums[:, i : i + 1])
            scaled = stat.tile([P, len(PIECES)], F32, name="scaled")
            neg_mean = stat.tile([P, 1], F32, name="neg_mean")
            nc.scalar.activation(scaled[:], osums[:], ACT.Identity, scale=-1.0 / N, accum_out=neg_mean[:])
            squares = work.tile([P, N], F32, name="squares")
            ssq = stat.tile([P, 1], F32, name="ssq")
            nc.scalar.activation(squares[:], o_sb[:], ACT.Square, bias=neg_mean[:], accum_out=ssq[:])
            slope = work.tile([P, N], F32, name="slope")
            if cb < VECTOR_MAKES_SLOPE_BELOW:
                scaled_up = stat.tile([P, len(PIECES)], F32, name="scaled_up")
                mean = stat.tile([P, 1], F32, name="mean")
                nc.scalar.activation(scaled_up[:], osums[:], ACT.Identity, scale=1.0 / N, accum_out=mean[:])
                nc.vector.tensor_scalar(slope[:], o_sb[:], mean[:], NEG_SLOPE, op0=ALU.is_ge, op1=ALU.max)
            rstd = stat.tile([P, 1], F32, name="rstd")
            nc.scalar.activation(rstd[:], ssq[:], ACT.Abs_reciprocal_sqrt, bias=eps[:], scale=1.0 / N)
            z = work.tile([P, N], F32, name="z")
            make_z(z, o_sb, neg_mean, rstd, slice(0, N))
            if cb >= VECTOR_MAKES_SLOPE_BELOW:
                make_slope(slope, o_sb, neg_mean, slice(0, N))
            nc.vector.tensor_tensor(window[cb][:].indirect(offsets[:]), z[:], slope[:], ALU.mult)
            nc.sync.dma_start(out_rows[cb], window[cb][:])

        def attn_blocks(attn_bf):
            return [attn_bf[:, nb * P : (nb + 1) * P] for nb in range(NB)]

        def attnT_block(jb):
            return attnT[jb // QB][:, :, (jb % QB) * P : (jb % QB + 1) * P]

        waiting = {}
        for jb in range(NB):
            if jb == 0:
                flipping, target = flip_start(wh_blocks(CB - 1), LATE), whT_block(CB - 1)
            elif jb >= AHEAD:
                flipping, target = flip_start(attn_blocks(waiting.pop(jb - AHEAD)), LATE), attnT_block(jb - AHEAD)
            else:
                flipping = None
            waiting[jb], last_total = scores(jb, flipping)
            if flipping is not None:
                flip_done(flipping, target)
        unused = stat.tile([P, 1], F32, name="unused")
        nc.scalar.activation(unused[:], last_total[:], ACT.Abs_reciprocal_sqrt)
        o_first = []
        for i, piece in enumerate(FIRST_PIECES):
            jb = NB - AHEAD + i
            flipping = flip_start(attn_blocks(waiting.pop(jb)), (LATE, EARLY)[i]) if jb < NB else None
            o_first.append(attend(0, piece, flipping))
            if flipping is not None:
                flip_done(flipping, attnT_block(jb))
        place(0, o_first)
        for cb in range(1, CB):
            place(cb, [attend(cb, piece) for piece in PIECES])
